import numpy as np
import ml_dtypes


def mxq(x, axis, fmt="e4m3"):
    dtype, down = {"e4m3": (ml_dtypes.float8_e4m3fn, 7), "e5m2": (ml_dtypes.float8_e5m2, 14)}[fmt]
    v = np.moveaxis(np.asarray(x, np.float32).astype(ml_dtypes.bfloat16).astype(np.float64), axis, -1)
    blocks = v.reshape(v.shape[:-1] + (-1, 32))
    amax = np.abs(blocks).max(-1, keepdims=True)
    byte = np.maximum(np.where(amax > 0, np.frexp(amax)[1] - 1 + 127, 0) - down, 1)
    scale = np.exp2(byte - 127.0)
    codes = (blocks / scale).astype(np.float32).astype(dtype).astype(np.float64)
    return np.moveaxis((codes * scale).reshape(v.shape), -1, axis)


WIDE = False


def mx_kscale(k):
    if not WIDE:
        return np.ones(k)
    levels = np.array([10, -10, 5, -5, 0])
    if k % 512:
        return np.exp2(np.random.permutation(np.resize(levels, k // 32))).repeat(32)
    a = np.empty((k // 512, 16))
    for p in range(k // 512):
        a[p, :8] = np.random.permutation(np.resize(levels, 8))
        for g in range(8):
            far = levels[np.abs(levels - a[p, g]) >= 10]
            a[p, g + 8] = far[np.random.randint(len(far))]
    return np.exp2(a.ravel()).repeat(32)


BF16 = ml_dtypes.bfloat16


def bf(x):
    return np.asarray(x, np.float32).astype(BF16)


def f64(x):
    return np.asarray(x).astype(np.float64)


N, CIN, COUT, V, T, S = 2, 1024, 64, 64, 64, 8
EPS = 1e-5
KG = S * V


def setup_inputs():
    r = np.random.standard_normal
    c = mx_kscale(CIN)
    g = mx_kscale(KG).reshape(S, V)
    return {"ada_A": bf(r((N, CIN, V, V)) * c[None, :, None, None]),
            "ada_w": bf(r((S, COUT, CIN)) / np.sqrt(CIN) / c),
            "ada_b": bf(r((S, COUT)) * 0.3),
            "PA": bf(r((S, V, V)) * 2.0 / np.sqrt(KG) * g[:, None, :]),
            "feat": bf(r((S, N, COUT, V, T)) / g[:, None, None, :, None]),
            "bn_gamma": bf(1.0 + 0.1 * r(COUT)),
            "bn_beta": bf(0.3 * r(COUT)),
            "bn_mean": bf(0.3 * r(COUT)),
            "bn_var": bf(np.abs(r(COUT)) + 1.0),
            "res": bf(r((N, COUT, V, T)) * 0.9)}


def reference(ada_A, ada_w, ada_b, PA, feat, bn_gamma, bn_beta, bn_mean, bn_var, res):
    wq = mxq(f64(ada_w).reshape(S * COUT, CIN), 1, "e4m3")
    aq = mxq(f64(ada_A).reshape(N, CIN, V * V), 1, "e4m3")
    adaA = (wq @ aq).reshape(N, S, COUT, V, V).transpose(1, 0, 2, 3, 4) + f64(ada_b)[:, None, :, None, None]
    A_full = adaA * f64(PA)[:, None, None, :, :]
    Ag = A_full.transpose(1, 2, 3, 0, 4).reshape(N, COUT, V, KG)
    Fg = f64(feat).transpose(1, 2, 0, 3, 4).reshape(N, COUT, KG, T)
    y = mxq(Ag, 3, "e4m3") @ mxq(Fg, 2, "e4m3")
    scale = f64(bn_gamma) / np.sqrt(f64(bn_var) + EPS)
    z = (y - f64(bn_mean)[:, None, None]) * scale[:, None, None] + f64(bn_beta)[:, None, None]
    return np.maximum(z + f64(res), 0.0)

@@ -1,0 +1,416 @@
+from contextlib import ExitStack
+
+import concourse.mybir as mybir
+from concourse.masks import make_identity
+
+F32 = mybir.dt.float32
+BF16 = mybir.dt.bfloat16
+U32 = mybir.dt.uint32
+U8 = mybir.dt.uint8
+FP8X4 = mybir.dt.float8_e4m3fn_x4
+ACT = mybir.ActivationFunctionType
+ALU = mybir.AluOpType
+
+N, CIN, COUT, V, T, S = 2, 1024, 64, 64, 64, 8
+EPS = 1e-5
+FLOPS = 2 * N * S * COUT * CIN * V * V + 2 * N * COUT * V * S * V * T
+
+P = 128
+PACK = 4
+K_PASS = P * PACK
+C_PASSES = CIN // K_PASS
+SO = S * COUT
+VU = 32
+UNITS = N * V // VU
+W4 = V // PACK
+QUAD = 4
+QUADS = W4 // QUAD
+ITEM = QUAD * VU * PACK
+S_BANK = 2
+Q_BANKS = S // S_BANK
+O_GROUP = 8
+GROUPS = COUT // O_GROUP
+O_LOAD = 32
+PAIRS = O_GROUP // 2
+VECTOR_V_ALONE = 24
+VECTOR_V = 14
+VECTOR_O = 4
+
+
+def tile_multiscale_gcn_pa_t_kernel(
+    tc, ada_A, ada_w, ada_b, PA, feat, bn_gamma, bn_beta, bn_mean, bn_var, res, out
+):
+    nc = tc.nc
+    with ExitStack() as ctx:
+        const = ctx.enter_context(tc.tile_pool(name="const", bufs=1))
+        raw_pool = ctx.enter_context(tc.tile_pool(name="raw", bufs=3))
+        grouped_pool = ctx.enter_context(tc.tile_pool(name="grouped", bufs=2))
+        c0_pool = ctx.enter_context(tc.tile_pool(name="c0", bufs=4))
+        c1_pool = ctx.enter_context(tc.tile_pool(name="c1", bufs=2))
+        x_pool = ctx.enter_context(tc.tile_pool(name="x", bufs=2))
+        a_pool = ctx.enter_context(tc.tile_pool(name="a", bufs=1))
+        ac_pool = ctx.enter_context(tc.tile_pool(name="ac", bufs=2))
+        f_raw_pool = ctx.enter_context(tc.tile_pool(name="f_raw", bufs=2))
+        f_code_pool = ctx.enter_context(tc.tile_pool(name="f_codes", bufs=3))
+        z_pool = ctx.enter_context(tc.tile_pool(name="z", bufs=3))
+        ps_mx = ctx.enter_context(tc.psum_pool(name="ps_mx", bufs=4))
+        ps_turn = ctx.enter_context(tc.psum_pool(name="ps_turn", bufs=4))
+        ctx.enter_context(tc.manual_schedule())
+
+        def load_ada(unit, c):
+            n, h = divmod(unit, V // VU)
+            raw = raw_pool.tile([P, PACK, VU * V], BF16, tag="raw")
+            nc.sync.dma_start(
+                out=raw[:],
+                in_=ada_A[n, K_PASS * c : K_PASS * (c + 1), VU * h : VU * (h + 1), :].rearrange(
+                    "(p t) v w -> p t (v w)", t=PACK
+                ),
+            )
+            return raw
+
+        f_raws = {}
+
+        def load_feat(index, s):
+            n, part = divmod(index, COUT // O_LOAD)
+            if s == 0:
+                f_raw = f_raw_pool.tile([P, O_LOAD, PACK, T], BF16, tag="f_raw", align_bytes=64)
+                f_raws[index] = f_raw
+            nc.scalar.dma_start(
+                out=f_raws[index][W4 * s : W4 * (s + 1)].rearrange("q o j t -> q o (j t)"),
+                in_=feat[s, n, O_LOAD * part : O_LOAD * (part + 1), :, :].rearrange(
+                    "o (q j) t -> q o (j t)", j=PACK
+                ),
+            )
+
+        raws = {(0, 0): load_ada(0, 0)}
+        w_raw = f_raw_pool.tile([P, PACK, CIN], BF16, tag="f_raw", align_bytes=64)
+        nc.sync.dma_start(
+            out=w_raw[:], in_=ada_w.rearrange("(g x) o i -> (x o) g i", x=S_BANK)
+        )
+        raws[(0, 1)] = load_ada(0, 1)
+        raws[(1, 0)] = load_ada(1, 0)
+
+        b_raw = const.tile([P, COUT], BF16)
+        for s in range(S):
+            nc.sync.dma_start(
+                out=b_raw[W4 * s : W4 * (s + 1), :], in_=ada_b[s].partition_broadcast(W4)
+            )
+        pa_raw = const.tile([P, S * V], BF16)
+        for half in range(2):
+            nc.sync.dma_start(
+                out=pa_raw[V * half : V * (half + 1), :].rearrange("v (s w) -> v s w", s=S),
+                in_=PA.rearrange("s v w -> v s w"),
+            )
+        bn_raw = const.tile([P, 4, COUT], BF16)
+        for i, vec in enumerate((bn_gamma, bn_beta, bn_mean, bn_var)):
+            nc.sync.dma_start(out=bn_raw[:, i, :], in_=vec.partition_broadcast(P))
+        res_view = res.rearrange("n (a h) v t -> (h v) n a t", h=2)
+        out_view = out.rearrange("n (a h) v t -> (h v) n a t", h=2)
+
+        ident = const.tile([P, P], F32)
+        make_identity(nc, ident[:])
+        warm = const.tile([P, 1], F32)
+        nc.vector.memset(warm[:], 1.0)
+        nc.scalar.activation(out=warm[:], in_=warm[:], func=ACT.Sqrt)
+
+        def regroup_ada(raw, quad, cut):
+            grouped = grouped_pool.tile([P, QUAD, VU, PACK * PACK], BF16, tag="grouped", align_bytes=64)
+            dst = grouped[:].rearrange("p q v (j t) -> p v q t j", t=PACK)
+            src = raw[:].rearrange("p t (v k j) -> p v k t j", v=VU, j=PACK)[
+                :, :, QUAD * quad : QUAD * (quad + 1)
+            ]
+            nc.scalar.copy(out=dst[:, cut:], in_=src[:, cut:])
+            nc.vector.tensor_copy(out=dst[:, :cut], in_=src[:, :cut])
+            return grouped
+
+        def regroup_feat(f_raw, first_o, cut):
+            f_grouped = grouped_pool.tile([P, O_GROUP, T // 4, 4 * PACK], BF16, tag="f_grouped", align_bytes=64)
+            dst = f_grouped[:].rearrange("p o k (i j) -> p o k j i", j=PACK)
+            src = f_raw[:, first_o : first_o + O_GROUP].rearrange("p o j (k i) -> p o k j i", i=4)
+            nc.scalar.copy(out=dst[:, cut:], in_=src[:, cut:])
+            if cut > 0:
+                nc.vector.tensor_copy(out=dst[:, :cut], in_=src[:, :cut])
+            return f_grouped
+
+        def quantise(grouped, codes, scales):
+            nc.vector.quantize_mx(out=codes.bitcast(FP8X4), scales=scales, in_=grouped)
+
+        w_words = w_raw[:].bitcast(F32).rearrange("m g (c p u) -> m g c u p", c=C_PASSES, u=2)
+        w_grouped = f_raw_pool.tile([P, C_PASSES * SO, PACK], BF16, tag="f_raw", align_bytes=64)
+        w_grouped_words = (
+            w_grouped[:]
+            .rearrange("p w j -> p (w j)")
+            .bitcast(F32)
+            .rearrange("p (c g m u) -> p c g m u", c=C_PASSES, g=PACK, u=2)
+        )
+        w_codes = const.tile([P, C_PASSES, SO], U32, align_bytes=64)
+        w_scales = const.tile([P, C_PASSES, SO], U8, align_bytes=64)
+
+        def prepare_w():
+            for c in range(C_PASSES):
+                for g_pair in range(2):
+                    w_turned = ps_turn.tile([P, 4, P], F32, tag="turned")
+                    for g_low in range(2):
+                        for u in range(2):
+                            nc.tensor.transpose(
+                                w_turned[:, 2 * g_low + u, :],
+                                w_words[:, 2 * g_pair + g_low, c, u, :],
+                                ident[:],
+                            )
+                    copy_out = nc.vector.tensor_copy if g_pair == 0 else nc.scalar.copy
+                    copy_out(
+                        out=w_grouped_words[:, c, 2 * g_pair : 2 * g_pair + 2, :, :],
+                        in_=w_turned[:].rearrange("p (g u) m -> p g m u", u=2),
+                    )
+
+        def quantise_w():
+            quantise(
+                w_grouped[:].rearrange("p w j -> p (w j)"),
+                w_codes[:].rearrange("p c m -> p (c m)"),
+                w_scales[:].rearrange("p c m -> p (c m)"),
+            )
+
+        pa_sorted = grouped_pool.tile([P, PACK, P], F32, tag="f_grouped", align_bytes=64)
+        pa_t = const.tile([P, V, PACK], F32)
+        b_col = const.tile([P, COUT], F32)
+
+        def prepare_pa():
+            nc.vector.tensor_copy(out=pa_sorted[:], in_=pa_raw[:].rearrange("p (k j) -> p j k", j=PACK))
+            nc.vector.tensor_copy(out=b_col[:], in_=b_raw[:])
+            pa_turned = ps_turn.tile([P, 4, P], F32, tag="turned")
+            for j in range(PACK):
+                nc.tensor.transpose(pa_turned[:, j, :], pa_sorted[:, j, :], ident[:])
+            nc.vector.tensor_copy(
+                out=pa_t[:], in_=pa_turned[:, :, 0:V].rearrange("p j v -> p v j")
+            )
+
+        bn_f = const.tile([P, 4, COUT], F32)
+        rstd = const.tile([P, COUT], F32)
+        scale_all = const.tile([P, COUT], F32)
+        shift_all = const.tile([P, COUT], F32)
+        scale_col = const.tile([P, COUT // 2], F32)
+        shift_col = const.tile([P, COUT // 2], F32)
+
+        def prepare_bn():
+            nc.vector.tensor_copy(out=bn_f[:], in_=bn_raw[:])
+            nc.vector.tensor_scalar_add(out=rstd[:], in0=bn_f[:, 3, :], scalar1=EPS)
+            nc.scalar.activation(out=rstd[:], in_=rstd[:], func=ACT.Sqrt)
+            nc.vector.reciprocal(out=rstd[:], in_=rstd[:])
+            nc.vector.tensor_mul(out=scale_all[:], in0=bn_f[:, 0, :], in1=rstd[:])
+            nc.vector.tensor_mul(out=shift_all[:], in0=bn_f[:, 2, :], in1=scale_all[:])
+            nc.vector.tensor_sub(out=shift_all[:], in0=bn_f[:, 1, :], in1=shift_all[:])
+            for h in range(2):
+                rows = slice(V * h, V * (h + 1))
+                for col, full in ((scale_col, scale_all), (shift_col, shift_all)):
+                    nc.vector.tensor_copy(
+                        out=col[rows, :],
+                        in_=full[rows, :].rearrange("p (a h) -> p h a", h=2)[:, h, :],
+                    )
+
+        c0_codes, c1_codes = {}, {}
+
+        def quantise_ada(c, quad, grouped):
+            pool = c1_pool if c else c0_pool
+            codes = pool.tile([P, ITEM], U32, tag="codes", align_bytes=64)
+            scales = pool.tile([P, ITEM], U8, tag="scales", align_bytes=64)
+            quantise(grouped[:].rearrange("p q v j -> p (q v j)"), codes[:], scales[:])
+            (c1_codes if c else c0_codes)[quad] = (codes, scales)
+
+        def first_matmul(quad, banks):
+            unit, k = divmod(quad, QUADS)
+            for bank in banks:
+                acc = ps_mx.tile([P, QUAD, S_BANK * COUT], F32, tag="mx")
+                n_cols = slice(P * bank, P * (bank + 1))
+                for q in range(QUAD):
+                    m_cols = slice(P * q, P * (q + 1))
+                    for c, (codes, scales) in enumerate((c0_codes[quad], c1_codes[quad])):
+                        nc.tensor.matmul_mx(
+                            out=acc[:, q, :],
+                            lhsT=codes[:, m_cols].bitcast(FP8X4),
+                            lhsT_scale=scales[:, m_cols],
+                            rhs=w_codes[:, c, n_cols].bitcast(FP8X4),
+                            rhs_scale=w_scales[:, c, n_cols],
+                            start=(c == 0),
+                            stop=(c == C_PASSES - 1),
+                        )
+                nc.scalar.copy(
+                    out=x_tiles[unit][
+                        :, :, S_BANK * bank : S_BANK * (bank + 1), QUAD * k : QUAD * (k + 1)
+                    ],
+                    in_=acc[:].rearrange("p w (s o) -> p o s w", s=S_BANK),
+                )
+
+        def turn(unit, group):
+            banks = []
+            for half in range(2):
+                turned = ps_turn.tile([P, 4, P], F32, tag="turned")
+                for i in range(4):
+                    nc.tensor.transpose(
+                        turned[:, i, :],
+                        x_tiles[unit][:, O_GROUP * group + 4 * half + i, :, :].rearrange("p s w -> p (s w)"),
+                        ident[:],
+                    )
+                banks.append(turned)
+            return banks
+
+        def modulate(unit, group, banks, a_in):
+            v0 = VU * (unit % 2)
+            for half in range(2):
+                for i in range(4):
+                    o = O_GROUP * group + 4 * half + i
+                    nc.vector.scalar_tensor_tensor(
+                        out=a_in[:, o, v0 : v0 + VU, :].rearrange("p v j -> p (v j)"),
+                        in0=banks[half][:, i, :],
+                        scalar=b_col[:, o : o + 1],
+                        in1=pa_t[:, v0 : v0 + VU, :].rearrange("p v j -> p (v j)"),
+                        op0=ALU.add,
+                        op1=ALU.mult,
+                    )
+
+        def quantise_a(group, a_in):
+            codes = ac_pool.tile([P, O_GROUP * V], U32, tag="codes", align_bytes=64)
+            scales = ac_pool.tile([P, O_GROUP * V], U8, tag="scales", align_bytes=64)
+            quantise(
+                a_in[:, O_GROUP * group : O_GROUP * (group + 1)].rearrange("p o v j -> p (o v j)"),
+                codes[:],
+                scales[:],
+            )
+            return codes, scales
+
+        def quantise_feat(f_grouped):
+            codes = f_code_pool.tile([P, O_GROUP * T], U32, tag="codes", align_bytes=64)
+            scales = f_code_pool.tile([P, O_GROUP * T], U8, tag="scales", align_bytes=64)
+            quantise(f_grouped[:].rearrange("p o k j -> p (o k j)"), codes[:], scales[:])
+            return codes, scales
+
+        def second_matmul(group, a_codes, f_codes):
+            y_ps = ps_mx.tile([P, PAIRS, P], F32, tag="mx")
+            z = z_pool.tile([P, PAIRS, T], F32)
+            for pair in range(PAIRS):
+                cols = slice(P * pair, P * (pair + 1))
+                nc.tensor.matmul_mx(
+                    out=y_ps[:, pair, :],
+                    lhsT=a_codes[0][:, cols].bitcast(FP8X4),
+                    lhsT_scale=a_codes[1][:, cols],
+                    rhs=f_codes[0][:, cols].bitcast(FP8X4),
+                    rhs_scale=f_codes[1][:, cols],
+                    start=True,
+                    stop=True,
+                )
+            for pair in range(PAIRS):
+                a = PAIRS * group + pair
+                for h in range(2):
+                    rows = slice(V * h, V * (h + 1))
+                    nc.scalar.activation(
+                        out=z[rows, pair, :],
+                        in_=y_ps[rows, pair, T * h : T * (h + 1)],
+                        func=ACT.Identity,
+                        bias=shift_col[rows, a : a + 1],
+                        scale=scale_col[rows, a : a + 1],
+                    )
+            return z
+
+        def finish(n, group, z):
+            a0 = PAIRS * group
+            nc.vector.tensor_add(out=z[:], in0=z[:], in1=res_tiles[n][:, a0 : a0 + PAIRS, :])
+            nc.vector.tensor_scalar_max(out=z[:], in0=z[:], scalar1=0.0)
+            nc.sync.dma_start(out=out_view[:, n, a0 : a0 + PAIRS, :], in_=z[:])
+
+        all_quads = UNITS * QUADS
+        items = [(0, 0), (0, 1)]
+        for i in range(all_quads):
+            items.append((0, i + 2) if i + 2 < all_quads else None)
+            items.append((1, i))
+        matmul_at = {}
+        for i in range(all_quads):
+            done = items.index((1, i)) + 1
+            matmul_at[done + 1] = (i, (0, 1))
+            matmul_at[done + 2] = (i, (2, 3))
+        first_turn = [items.index((1, QUADS * (u + 1) - 1)) + 4 for u in range(UNITS)]
+        turn_at = {}
+        for u in range(UNITS):
+            for g in range(GROUPS):
+                turn_at[first_turn[u] + g] = (u, g)
+        multiply_at = {}
+        for n in range(N):
+            for g in range(GROUPS):
+                multiply_at[first_turn[2 * n + 1] + g + 2] = (n, g)
+        feat_at = {step - 2: item for step, item in multiply_at.items()}
+        feat_load_at = {}
+        for index, first in enumerate((2, 10, first_turn[1] + 5, first_turn[1] + 9)):
+            for s in range(S):
+                feat_load_at.setdefault(first + s, []).append((index, s))
+        ada_load_at = {}
+        for u in range(1, UNITS):
+            if u > 1:
+                ada_load_at[items.index((1, QUADS * (u - 1) - 1)) + 1] = (u, 0)
+            ada_load_at[items.index((0, QUADS * u - 1)) + 1] = (u, 1)
+
+        res_load_at = {first_turn[0] - 4: 0, max(step for step, (n, g) in multiply_at.items() if n == 0) + 2: 1}
+        res_tiles = {}
+        x_tiles = {}
+        a_in = None
+        grouped = None
+        f_grouped = None
+        f_codes = {}
+        a_codes = {}
+        unfinished = None
+        last = max(multiply_at)
+        for step in range(last + 2):
+            if step in ada_load_at:
+                raws[ada_load_at[step]] = load_ada(*ada_load_at[step])
+            if step in res_load_at:
+                n = res_load_at[step]
+                res_sb = const.tile([P, COUT // 2, T], BF16)
+                nc.sync.dma_start(out=res_sb[:], in_=res_view[:, n, :, :])
+                res_tiles[n] = res_sb
+            if grouped is not None:
+                quantise_ada(*items[step - 1], grouped)
+                grouped = None
+            if f_grouped is not None:
+                f_codes[feat_at[step - 1]] = quantise_feat(f_grouped)
+                f_grouped = None
+            banks = turn(*turn_at[step]) if step in turn_at else None
+            if step < len(items) and items[step] is not None:
+                c, quad = items[step]
+                cut = VECTOR_V_ALONE if step < first_turn[0] else VECTOR_V
+                grouped = regroup_ada(raws[(quad // QUADS, c)], quad % QUADS, cut)
+            if step in feat_at:
+                n, g = feat_at[step]
+                per_load = O_LOAD // O_GROUP
+                f_grouped = regroup_feat(
+                    f_raws[n * (COUT // O_LOAD) + g // per_load],
+                    O_GROUP * (g % per_load),
+                    VECTOR_O if n == 0 else 0,
+                )
+            if step == 1:
+                prepare_w()
+            if step == 2:
+                quantise_w()
+            if step == first_turn[0] - 4:
+                prepare_pa()
+            if step == first_turn[0] - 2:
+                prepare_bn()
+            if unfinished is not None:
+                finish(*unfinished)
+                unfinished = None
+            if step - 1 in turn_at and turn_at[step - 1][0] % 2 == 1:
+                unit, g = turn_at[step - 1]
+                a_codes[(unit // 2, g)] = quantise_a(g, a_in)
+            if banks is not None:
+                unit, g = turn_at[step]
+                if unit % 2 == 0 and g == 0:
+                    a_in = a_pool.tile([P, COUT, V, PACK], BF16, align_bytes=64)
+                modulate(unit, g, banks, a_in)
+            if step in matmul_at:
+                quad, quad_banks = matmul_at[step]
+                if quad % QUADS == 0 and quad_banks[0] == 0:
+                    x_sb = x_pool.tile([P, COUT, S, W4], F32)
+                    x_tiles[quad // QUADS] = x_sb
+                first_matmul(quad, quad_banks)
+            if step in multiply_at:
+                n, g = multiply_at[step]
+                z = second_matmul(g, a_codes[(n, g)], f_codes[(n, g)])
+                unfinished = (n, g, z)
+            for index, s in feat_load_at.get(step, []):
+                load_feat(index, s)

@@ -30,11 +30,13 @@ S_BANK = 2
 Q_BANKS = S // S_BANK
 O_GROUP = 8
 GROUPS = COUT // O_GROUP
-O_LOAD = 32
 PAIRS = O_GROUP // 2
 VECTOR_V_ALONE = 24
 VECTOR_V = 14
-VECTOR_O = 4
+KIB = 1024
+F_NAT_AT, F_GROUPED_AT = 0, 72 * KIB
+F_CODES_AT, F_SCALES_AT, X_AT, A_AT = 0, 32 * KIB, (40 * KIB, 72 * KIB), 104 * KIB
+W_RAW_AT, W_GROUPED_AT = 72 * KIB, 80 * KIB
 
 
 def tile_multiscale_gcn_pa_t_kernel(
@@ -47,11 +49,8 @@ def tile_multiscale_gcn_pa_t_kernel(
         grouped_pool = ctx.enter_context(tc.tile_pool(name="grouped", bufs=2))
         c0_pool = ctx.enter_context(tc.tile_pool(name="c0", bufs=4))
         c1_pool = ctx.enter_context(tc.tile_pool(name="c1", bufs=2))
-        x_pool = ctx.enter_context(tc.tile_pool(name="x", bufs=2))
-        a_pool = ctx.enter_context(tc.tile_pool(name="a", bufs=1))
+        big = ctx.enter_context(tc.tile_pool(name="big", bufs=1))
         ac_pool = ctx.enter_context(tc.tile_pool(name="ac", bufs=2))
-        f_raw_pool = ctx.enter_context(tc.tile_pool(name="f_raw", bufs=2))
-        f_code_pool = ctx.enter_context(tc.tile_pool(name="f_codes", bufs=3))
         z_pool = ctx.enter_context(tc.tile_pool(name="z", bufs=3))
         ps_mx = ctx.enter_context(tc.psum_pool(name="ps_mx", bufs=4))
         ps_turn = ctx.enter_context(tc.psum_pool(name="ps_turn", bufs=4))
@@ -68,25 +67,14 @@ def tile_multiscale_gcn_pa_t_kernel(
             )
             return raw
 
-        f_raws = {}
-
-        def load_feat(index, s):
-            n, part = divmod(index, COUT // O_LOAD)
-            if s == 0:
-                f_raw = f_raw_pool.tile([P, O_LOAD, PACK, T], BF16, tag="f_raw", align_bytes=64)
-                f_raws[index] = f_raw
-            nc.scalar.dma_start(
-                out=f_raws[index][W4 * s : W4 * (s + 1)].rearrange("q o j t -> q o (j t)"),
-                in_=feat[s, n, O_LOAD * part : O_LOAD * (part + 1), :, :].rearrange(
-                    "o (q j) t -> q o (j t)", j=PACK
-                ),
-            )
-
-        raws = {(0, 0): load_ada(0, 0)}
-        w_raw = f_raw_pool.tile([P, PACK, CIN], BF16, tag="f_raw", align_bytes=64)
+        w_raw = big.tile([P, PACK, CIN], BF16, align_bytes=64, offset=W_RAW_AT)
         nc.sync.dma_start(
             out=w_raw[:], in_=ada_w.rearrange("(g x) o i -> (x o) g i", x=S_BANK)
         )
+        f_nat = big.tile([P, S, V * T], BF16, align_bytes=64, offset=F_NAT_AT)
+        for s in range(S):
+            nc.sync.dma_start(out=f_nat[:, s, :], in_=feat[s].rearrange("n o w t -> (n o) (w t)"))
+        raws = {(0, 0): load_ada(0, 0)}
         raws[(0, 1)] = load_ada(0, 1)
         raws[(1, 0)] = load_ada(1, 0)
 
@@ -123,20 +111,11 @@ def tile_multiscale_gcn_pa_t_kernel(
             nc.vector.tensor_copy(out=dst[:, :cut], in_=src[:, :cut])
             return grouped
 
-        def regroup_feat(f_raw, first_o, cut):
-            f_grouped = grouped_pool.tile([P, O_GROUP, T // 4, 4 * PACK], BF16, tag="f_grouped", align_bytes=64)
-            dst = f_grouped[:].rearrange("p o k (i j) -> p o k j i", j=PACK)
-            src = f_raw[:, first_o : first_o + O_GROUP].rearrange("p o j (k i) -> p o k j i", i=4)
-            nc.scalar.copy(out=dst[:, cut:], in_=src[:, cut:])
-            if cut > 0:
-                nc.vector.tensor_copy(out=dst[:, :cut], in_=src[:, :cut])
-            return f_grouped
-
         def quantise(grouped, codes, scales):
             nc.vector.quantize_mx(out=codes.bitcast(FP8X4), scales=scales, in_=grouped)
 
         w_words = w_raw[:].bitcast(F32).rearrange("m g (c p u) -> m g c u p", c=C_PASSES, u=2)
-        w_grouped = f_raw_pool.tile([P, C_PASSES * SO, PACK], BF16, tag="f_raw", align_bytes=64)
+        w_grouped = big.tile([P, C_PASSES * SO, PACK], BF16, align_bytes=64, offset=W_GROUPED_AT)
         w_grouped_words = (
             w_grouped[:]
             .rearrange("p w j -> p (w j)")
@@ -170,7 +149,7 @@ def tile_multiscale_gcn_pa_t_kernel(
                 w_scales[:].rearrange("p c m -> p (c m)"),
             )
 
-        pa_sorted = grouped_pool.tile([P, PACK, P], F32, tag="f_grouped", align_bytes=64)
+        pa_sorted = const.tile([P, PACK, P], F32)
         pa_t = const.tile([P, V, PACK], F32)
         b_col = const.tile([P, COUT], F32)
 
@@ -277,23 +256,46 @@ def tile_multiscale_gcn_pa_t_kernel(
             )
             return codes, scales
 
-        def quantise_feat(f_grouped):
-            codes = f_code_pool.tile([P, O_GROUP * T], U32, tag="codes", align_bytes=64)
-            scales = f_code_pool.tile([P, O_GROUP * T], U8, tag="scales", align_bytes=64)
-            quantise(f_grouped[:].rearrange("p o k j -> p (o k j)"), codes[:], scales[:])
-            return codes, scales
+        f_words = (
+            f_nat[:]
+            .rearrange("p s c -> p (s c)")
+            .bitcast(F32)
+            .rearrange("p (m j u) -> p j u m", j=PACK, u=T // 2)
+        )
+        def turn_feat(u):
+            turned = ps_turn.tile([P, PACK, P], F32, tag="turned")
+            for j in range(PACK):
+                nc.tensor.transpose(turned[:, j, :], f_words[:, j, u, :], ident[:])
+            copy_out = nc.vector.tensor_copy if u % 2 == 0 else nc.scalar.copy
+            copy_out(
+                out=f_grouped[:, :, 2 * u : 2 * u + 2, :].rearrange("p m e j -> p m j e"),
+                in_=turned[:]
+                .rearrange("p j m -> p (j m)")
+                .bitcast(BF16)
+                .rearrange("p (j m e) -> p m j e", j=PACK, e=2),
+            )
 
-        def second_matmul(group, a_codes, f_codes):
+        def quantise_feat(chunk):
+            cols = slice(O_GROUP * T * chunk, O_GROUP * T * (chunk + 1))
+            quantise(
+                f_grouped[:, O_GROUP * chunk : O_GROUP * (chunk + 1)].rearrange("p m t j -> p (m t j)"),
+                f_codes[:, cols],
+                f_scales[:, cols],
+            )
+
+        def second_matmul(n, group, a_codes):
             y_ps = ps_mx.tile([P, PAIRS, P], F32, tag="mx")
             z = z_pool.tile([P, PAIRS, T], F32)
             for pair in range(PAIRS):
                 cols = slice(P * pair, P * (pair + 1))
+                first = (COUT * n + O_GROUP * group) * T + P * pair
+                f_cols = slice(first, first + P)
                 nc.tensor.matmul_mx(
                     out=y_ps[:, pair, :],
                     lhsT=a_codes[0][:, cols].bitcast(FP8X4),
                     lhsT_scale=a_codes[1][:, cols],
-                    rhs=f_codes[0][:, cols].bitcast(FP8X4),
-                    rhs_scale=f_codes[1][:, cols],
+                    rhs=f_codes[:, f_cols].bitcast(FP8X4),
+                    rhs_scale=f_scales[:, f_cols],
                     start=True,
                     stop=True,
                 )
@@ -335,11 +337,6 @@ def tile_multiscale_gcn_pa_t_kernel(
         for n in range(N):
             for g in range(GROUPS):
                 multiply_at[first_turn[2 * n + 1] + g + 2] = (n, g)
-        feat_at = {step - 2: item for step, item in multiply_at.items()}
-        feat_load_at = {}
-        for index, first in enumerate((2, 10, first_turn[1] + 5, first_turn[1] + 9)):
-            for s in range(S):
-                feat_load_at.setdefault(first + s, []).append((index, s))
         ada_load_at = {}
         for u in range(1, UNITS):
             if u > 1:
@@ -351,12 +348,20 @@ def tile_multiscale_gcn_pa_t_kernel(
         x_tiles = {}
         a_in = None
         grouped = None
-        f_grouped = None
-        f_codes = {}
         a_codes = {}
         unfinished = None
         last = max(multiply_at)
+        prepare_w()
+        quantise_w()
+        f_grouped = big.tile([P, N * COUT, T, PACK], BF16, align_bytes=64, offset=F_GROUPED_AT)
+        for u in range(T // 2):
+            turn_feat(u)
+        f_codes = big.tile([P, N * COUT * T], U32, align_bytes=64, offset=F_CODES_AT)
+        f_scales = big.tile([P, N * COUT * T], U8, align_bytes=64, offset=F_SCALES_AT)
         for step in range(last + 2):
+            if step < N * COUT // O_GROUP // 2:
+                quantise_feat(2 * step)
+                quantise_feat(2 * step + 1)
             if step in ada_load_at:
                 raws[ada_load_at[step]] = load_ada(*ada_load_at[step])
             if step in res_load_at:
@@ -367,26 +372,12 @@ def tile_multiscale_gcn_pa_t_kernel(
             if grouped is not None:
                 quantise_ada(*items[step - 1], grouped)
                 grouped = None
-            if f_grouped is not None:
-                f_codes[feat_at[step - 1]] = quantise_feat(f_grouped)
-                f_grouped = None
             banks = turn(*turn_at[step]) if step in turn_at else None
             if step < len(items) and items[step] is not None:
                 c, quad = items[step]
-                cut = VECTOR_V_ALONE if step < first_turn[0] else VECTOR_V
+                alone = step < first_turn[0] and step >= N * COUT // O_GROUP // 2
+                cut = VECTOR_V_ALONE if alone else VECTOR_V
                 grouped = regroup_ada(raws[(quad // QUADS, c)], quad % QUADS, cut)
-            if step in feat_at:
-                n, g = feat_at[step]
-                per_load = O_LOAD // O_GROUP
-                f_grouped = regroup_feat(
-                    f_raws[n * (COUT // O_LOAD) + g // per_load],
-                    O_GROUP * (g % per_load),
-                    VECTOR_O if n == 0 else 0,
-                )
-            if step == 1:
-                prepare_w()
-            if step == 2:
-                quantise_w()
             if step == first_turn[0] - 4:
                 prepare_pa()
             if step == first_turn[0] - 2:
@@ -400,17 +391,16 @@ def tile_multiscale_gcn_pa_t_kernel(
             if banks is not None:
                 unit, g = turn_at[step]
                 if unit % 2 == 0 and g == 0:
-                    a_in = a_pool.tile([P, COUT, V, PACK], BF16, align_bytes=64)
+                    a_in = big.tile([P, COUT, V, PACK], BF16, align_bytes=64, offset=A_AT)
                 modulate(unit, g, banks, a_in)
             if step in matmul_at:
                 quad, quad_banks = matmul_at[step]
                 if quad % QUADS == 0 and quad_banks[0] == 0:
-                    x_sb = x_pool.tile([P, COUT, S, W4], F32)
-                    x_tiles[quad // QUADS] = x_sb
+                    unit = quad // QUADS
+                    x_sb = big.tile([P, COUT, S, W4], F32, tag=("x0", "x1")[unit % 2], align_bytes=64, offset=X_AT[unit % 2])
+                    x_tiles[unit] = x_sb
                 first_matmul(quad, quad_banks)
             if step in multiply_at:
                 n, g = multiply_at[step]
-                z = second_matmul(g, a_codes[(n, g)], f_codes[(n, g)])
+                z = second_matmul(n, g, a_codes[(n, g)])
                 unfinished = (n, g, z)
-            for index, s in feat_load_at.get(step, []):
-                load_feat(index, s)

@@ -34,9 +34,10 @@ PAIRS = O_GROUP // 2
 VECTOR_V_ALONE = 24
 VECTOR_V = 14
 KIB = 1024
-F_NAT_AT, F_GROUPED_AT = 0, 72 * KIB
-F_CODES_AT, F_SCALES_AT, X_AT, A_AT = 0, 32 * KIB, (40 * KIB, 72 * KIB), 104 * KIB
-W_RAW_AT, W_GROUPED_AT = 72 * KIB, 80 * KIB
+SORT_J = 3
+F_NAT_AT, F_SORTED_AT, F_GROUPED_AT = 0, 72 * KIB, 0
+F_CODES_AT, F_SCALES_AT, X_AT, A_AT = 72 * KIB, 64 * KIB, (104 * KIB, 32 * KIB), 0
+W_RAW_AT = 64 * KIB
 
 
 def tile_multiscale_gcn_pa_t_kernel(
@@ -115,18 +116,16 @@ def tile_multiscale_gcn_pa_t_kernel(
             nc.vector.quantize_mx(out=codes.bitcast(FP8X4), scales=scales, in_=grouped)
 
         w_words = w_raw[:].bitcast(F32).rearrange("m g (c p u) -> m g c u p", c=C_PASSES, u=2)
-        w_grouped = big.tile([P, C_PASSES * SO, PACK], BF16, align_bytes=64, offset=W_GROUPED_AT)
-        w_grouped_words = (
-            w_grouped[:]
-            .rearrange("p w j -> p (w j)")
-            .bitcast(F32)
-            .rearrange("p (c g m u) -> p c g m u", c=C_PASSES, g=PACK, u=2)
-        )
         w_codes = const.tile([P, C_PASSES, SO], U32, align_bytes=64)
         w_scales = const.tile([P, C_PASSES, SO], U8, align_bytes=64)
 
+        w_tiles = []
+
         def prepare_w():
             for c in range(C_PASSES):
+                w_grouped = grouped_pool.tile([P, SO * PACK], BF16, tag="grouped", align_bytes=64)
+                w_grouped_words = w_grouped[:].bitcast(F32).rearrange("p (g m u) -> p g m u", g=PACK, u=2)
+                w_tiles.append(w_grouped)
                 for g_pair in range(2):
                     w_turned = ps_turn.tile([P, 4, P], F32, tag="turned")
                     for g_low in range(2):
@@ -138,16 +137,13 @@ def tile_multiscale_gcn_pa_t_kernel(
                             )
                     copy_out = nc.vector.tensor_copy if g_pair == 0 else nc.scalar.copy
                     copy_out(
-                        out=w_grouped_words[:, c, 2 * g_pair : 2 * g_pair + 2, :, :],
+                        out=w_grouped_words[:, 2 * g_pair : 2 * g_pair + 2, :, :],
                         in_=w_turned[:].rearrange("p (g u) m -> p g m u", u=2),
                     )
 
         def quantise_w():
-            quantise(
-                w_grouped[:].rearrange("p w j -> p (w j)"),
-                w_codes[:].rearrange("p c m -> p (c m)"),
-                w_scales[:].rearrange("p c m -> p (c m)"),
-            )
+            for c in range(C_PASSES):
+                quantise(w_tiles[c][:], w_codes[:, c, :], w_scales[:, c, :])
 
         pa_sorted = const.tile([P, PACK, P], F32)
         pa_t = const.tile([P, V, PACK], F32)
@@ -256,16 +252,17 @@ def tile_multiscale_gcn_pa_t_kernel(
             )
             return codes, scales
 
-        f_words = (
-            f_nat[:]
-            .rearrange("p s c -> p (s c)")
-            .bitcast(F32)
-            .rearrange("p (m j u) -> p j u m", j=PACK, u=T // 2)
-        )
+        def sort_feat(s):
+            cut = SORT_J * T // 2
+            src = f_nat[:, s, :].bitcast(F32).rearrange("p (k q x) -> p k x q", k=W4 // 4, q=4)
+            dst = f_sorted[:, :, W4 * s : W4 * (s + 1)].rearrange("p x (k q) -> p k x q", q=4)
+            nc.vector.tensor_copy(out=dst[:, :, :cut], in_=src[:, :, :cut])
+            nc.scalar.copy(out=dst[:, :, cut:], in_=src[:, :, cut:])
+
         def turn_feat(u):
             turned = ps_turn.tile([P, PACK, P], F32, tag="turned")
             for j in range(PACK):
-                nc.tensor.transpose(turned[:, j, :], f_words[:, j, u, :], ident[:])
+                nc.tensor.transpose(turned[:, j, :], f_sorted[:, T // 2 * j + u, :], ident[:])
             copy_out = nc.vector.tensor_copy if u % 2 == 0 else nc.scalar.copy
             copy_out(
                 out=f_grouped[:, :, 2 * u : 2 * u + 2, :].rearrange("p m e j -> p m j e"),
@@ -353,6 +350,9 @@ def tile_multiscale_gcn_pa_t_kernel(
         last = max(multiply_at)
         prepare_w()
         quantise_w()
+        f_sorted = big.tile([P, PACK * T // 2, S * W4], F32, align_bytes=64, offset=F_SORTED_AT)
+        for s in range(S):
+            sort_feat(s)
         f_grouped = big.tile([P, N * COUT, T, PACK], BF16, align_bytes=64, offset=F_GROUPED_AT)
         for u in range(T // 2):
             turn_feat(u)

@@ -32,9 +32,13 @@ O_GROUP = 8
 GROUPS = COUT // O_GROUP
 PAIRS = O_GROUP // 2
 VECTOR_V_ALONE = 24
-VECTOR_V = 14
+VECTOR_V_FEAT = 10
+VECTOR_V = 16
 KIB = 1024
-SORT_J = 3
+SORT_LINE = 4
+SORT_V = 5
+W_AFTER = 4
+WARM = 4
 F_NAT_AT, F_SORTED_AT, F_GROUPED_AT = 0, 72 * KIB, 0
 F_CODES_AT, F_SCALES_AT, X_AT, A_AT = 72 * KIB, 64 * KIB, (104 * KIB, 32 * KIB), 0
 W_RAW_AT = 64 * KIB
@@ -69,11 +73,12 @@ def tile_multiscale_gcn_pa_t_kernel(
             return raw
 
         w_raw = big.tile([P, PACK, CIN], BF16, align_bytes=64, offset=W_RAW_AT)
-        nc.sync.dma_start(
-            out=w_raw[:], in_=ada_w.rearrange("(g x) o i -> (x o) g i", x=S_BANK)
-        )
         f_nat = big.tile([P, S, V * T], BF16, align_bytes=64, offset=F_NAT_AT)
         for s in range(S):
+            if s == W_AFTER:
+                nc.sync.dma_start(
+                    out=w_raw[:], in_=ada_w.rearrange("(g x) o i -> (x o) g i", x=S_BANK)
+                )
             nc.sync.dma_start(out=f_nat[:, s, :], in_=feat[s].rearrange("n o w t -> (n o) (w t)"))
         raws = {(0, 0): load_ada(0, 0)}
         raws[(0, 1)] = load_ada(0, 1)
@@ -253,23 +258,44 @@ def tile_multiscale_gcn_pa_t_kernel(
             return codes, scales
 
         def sort_feat(s):
-            cut = SORT_J * T // 2
-            src = f_nat[:, s, :].bitcast(F32).rearrange("p (k q x) -> p k x q", k=W4 // 4, q=4)
-            dst = f_sorted[:, :, W4 * s : W4 * (s + 1)].rearrange("p x (k q) -> p k x q", q=4)
-            nc.vector.tensor_copy(out=dst[:, :, :cut], in_=src[:, :, :cut])
-            nc.scalar.copy(out=dst[:, :, cut:], in_=src[:, :, cut:])
+            src = f_nat[:, s, :].rearrange(
+                "p (k q h e x i) -> p k h x q e i", k=W4 // SORT_LINE, q=SORT_LINE, h=2, e=2, i=4
+            )
+            dst = f_sorted[:, :, :, W4 * s : W4 * (s + 1), :].rearrange(
+                "p h (x i) (k q) e -> p k h x q e i", q=SORT_LINE, i=4
+            )
+            for piece in range(2 * W4 // SORT_LINE):
+                k, h = divmod(piece, 2)
+                copy = nc.vector.tensor_copy if piece < SORT_V else nc.scalar.copy
+                copy(out=dst[:, k, h], in_=src[:, k, h])
+
+        def warm_up():
+            bank = ps_mx.tile([P, 4, P], F32, tag="mx")
+            for i in range(WARM):
+                nc.tensor.matmul(
+                    bank[:].rearrange("p a b -> p (a b)"),
+                    lhsT=f_sorted[:, 1, T - 1, W4 * (S - 5) : W4 * (S - 1), :].rearrange("p m e -> p (m e)"),
+                    rhs=f_nat[:, S - 2, 0 : 4 * P],
+                    start=True,
+                    stop=True,
+                )
 
         def turn_feat(u):
-            turned = ps_turn.tile([P, PACK, P], F32, tag="turned")
-            for j in range(PACK):
-                nc.tensor.transpose(turned[:, j, :], f_sorted[:, T // 2 * j + u, :], ident[:])
+            if u % 2 == 0:
+                turned = ps_turn.tile([P, 4, P], F32, tag="turned")
+            else:
+                turned = ps_mx.tile([P, 4, P], F32, tag="mx")
+            words = f_sorted[:].rearrange("p h t m e -> p h t (m e)").bitcast(F32)
+            for i in range(2):
+                for h in range(2):
+                    nc.tensor.transpose(turned[:, 2 * i + h, :], words[:, h, 2 * u + i, :], ident[:])
             copy_out = nc.vector.tensor_copy if u % 2 == 0 else nc.scalar.copy
             copy_out(
-                out=f_grouped[:, :, 2 * u : 2 * u + 2, :].rearrange("p m e j -> p m j e"),
-                in_=turned[:]
-                .rearrange("p j m -> p (j m)")
-                .bitcast(BF16)
-                .rearrange("p (j m e) -> p m j e", j=PACK, e=2),
+                out=f_grouped[:]
+                .rearrange("p m t j -> p (m t j)")
+                .bitcast(F32)
+                .rearrange("p (m x) -> p m x", m=N * COUT)[:, :, 4 * u : 4 * (u + 1)],
+                in_=turned[:].rearrange("p x m -> p m x"),
             )
 
         def quantise_feat(chunk):
@@ -296,10 +322,10 @@ def tile_multiscale_gcn_pa_t_kernel(
                     start=True,
                     stop=True,
                 )
-            for pair in range(PAIRS):
-                a = PAIRS * group + pair
-                for h in range(2):
-                    rows = slice(V * h, V * (h + 1))
+            for h in range(2):
+                rows = slice(V * h, V * (h + 1))
+                for pair in range(PAIRS):
+                    a = PAIRS * group + pair
                     nc.scalar.activation(
                         out=z[rows, pair, :],
                         in_=y_ps[rows, pair, T * h : T * (h + 1)],
@@ -312,7 +338,13 @@ def tile_multiscale_gcn_pa_t_kernel(
         def finish(n, group, z):
             a0 = PAIRS * group
             nc.vector.tensor_add(out=z[:], in0=z[:], in1=res_tiles[n][:, a0 : a0 + PAIRS, :])
-            nc.vector.tensor_scalar_max(out=z[:], in0=z[:], scalar1=0.0)
+
+        def store(n, group, z):
+            a0 = PAIRS * group
+            if n == N - 1:
+                nc.scalar.activation(out=z[:], in_=z[:], func=ACT.Relu)
+            else:
+                nc.vector.tensor_scalar_max(out=z[:], in0=z[:], scalar1=0.0)
             nc.sync.dma_start(out=out_view[:, n, a0 : a0 + PAIRS, :], in_=z[:])
 
         all_quads = UNITS * QUADS
@@ -348,11 +380,14 @@ def tile_multiscale_gcn_pa_t_kernel(
         a_codes = {}
         unfinished = None
         last = max(multiply_at)
-        prepare_w()
-        quantise_w()
-        f_sorted = big.tile([P, PACK * T // 2, S * W4], F32, align_bytes=64, offset=F_SORTED_AT)
+        f_sorted = big.tile([P, 2, T, S * W4, 2], BF16, align_bytes=64, offset=F_SORTED_AT)
         for s in range(S):
             sort_feat(s)
+            if s == W_AFTER:
+                prepare_w()
+            if s == W_AFTER + 1:
+                quantise_w()
+        warm_up()
         f_grouped = big.tile([P, N * COUT, T, PACK], BF16, align_bytes=64, offset=F_GROUPED_AT)
         for u in range(T // 2):
             turn_feat(u)
@@ -375,16 +410,19 @@ def tile_multiscale_gcn_pa_t_kernel(
             banks = turn(*turn_at[step]) if step in turn_at else None
             if step < len(items) and items[step] is not None:
                 c, quad = items[step]
-                alone = step < first_turn[0] and step >= N * COUT // O_GROUP // 2
-                cut = VECTOR_V_ALONE if alone else VECTOR_V
+                if step < N * COUT // O_GROUP // 2:
+                    cut = VECTOR_V_FEAT
+                else:
+                    cut = VECTOR_V_ALONE if step < first_turn[0] else VECTOR_V
                 grouped = regroup_ada(raws[(quad // QUADS, c)], quad % QUADS, cut)
             if step == first_turn[0] - 4:
                 prepare_pa()
             if step == first_turn[0] - 2:
                 prepare_bn()
-            if unfinished is not None:
-                finish(*unfinished)
-                unfinished = None
+            to_store = unfinished
+            unfinished = None
+            if to_store is not None:
+                finish(*to_store)
             if step - 1 in turn_at and turn_at[step - 1][0] % 2 == 1:
                 unit, g = turn_at[step - 1]
                 a_codes[(unit // 2, g)] = quantise_a(g, a_in)
@@ -393,6 +431,8 @@ def tile_multiscale_gcn_pa_t_kernel(
                 if unit % 2 == 0 and g == 0:
                     a_in = big.tile([P, COUT, V, PACK], BF16, align_bytes=64, offset=A_AT)
                 modulate(unit, g, banks, a_in)
+            if to_store is not None:
+                store(*to_store)
             if step in matmul_at:
                 quad, quad_banks = matmul_at[step]
                 if quad % QUADS == 0 and quad_banks[0] == 0:

from contextlib import ExitStack

import concourse.mybir as mybir
from concourse.masks import make_identity

F32 = mybir.dt.float32
BF16 = mybir.dt.bfloat16
U32 = mybir.dt.uint32
U8 = mybir.dt.uint8
FP8X4 = mybir.dt.float8_e4m3fn_x4
ACT = mybir.ActivationFunctionType
ALU = mybir.AluOpType

N, CIN, COUT, V, T, S = 2, 1024, 64, 64, 64, 8
EPS = 1e-5
FLOPS = 2 * N * S * COUT * CIN * V * V + 2 * N * COUT * V * S * V * T

P = 128
PACK = 4
K_PASS = P * PACK
C_PASSES = CIN // K_PASS
SO = S * COUT
VU = 32
UNITS = N * V // VU
W4 = V // PACK
QUAD = 4
QUADS = W4 // QUAD
ITEM = QUAD * VU * PACK
S_BANK = 2
Q_BANKS = S // S_BANK
O_GROUP = 8
GROUPS = COUT // O_GROUP
PAIRS = O_GROUP // 2
VECTOR_V_ALONE = 24
VECTOR_V_FEAT = 10
VECTOR_V = 16
KIB = 1024
SORT_LINE = 4
SORT_V = 5
W_AFTER = 4
WARM = 4
F_NAT_AT, F_SORTED_AT, F_GROUPED_AT = 0, 72 * KIB, 0
F_CODES_AT, F_SCALES_AT, X_AT, A_AT = 72 * KIB, 64 * KIB, (104 * KIB, 32 * KIB), 0
W_RAW_AT = 64 * KIB


def tile_multiscale_gcn_pa_t_kernel(
    tc, ada_A, ada_w, ada_b, PA, feat, bn_gamma, bn_beta, bn_mean, bn_var, res, out
):
    nc = tc.nc
    with ExitStack() as ctx:
        const = ctx.enter_context(tc.tile_pool(name="const", bufs=1))
        raw_pool = ctx.enter_context(tc.tile_pool(name="raw", bufs=3))
        grouped_pool = ctx.enter_context(tc.tile_pool(name="grouped", bufs=2))
        c0_pool = ctx.enter_context(tc.tile_pool(name="c0", bufs=4))
        c1_pool = ctx.enter_context(tc.tile_pool(name="c1", bufs=2))
        big = ctx.enter_context(tc.tile_pool(name="big", bufs=1))
        ac_pool = ctx.enter_context(tc.tile_pool(name="ac", bufs=2))
        z_pool = ctx.enter_context(tc.tile_pool(name="z", bufs=3))
        ps_mx = ctx.enter_context(tc.psum_pool(name="ps_mx", bufs=4))
        ps_turn = ctx.enter_context(tc.psum_pool(name="ps_turn", bufs=4))
        ctx.enter_context(tc.manual_schedule())

        def load_ada(unit, c):
            n, h = divmod(unit, V // VU)
            raw = raw_pool.tile([P, PACK, VU * V], BF16, tag="raw")
            nc.sync.dma_start(
                out=raw[:],
                in_=ada_A[n, K_PASS * c : K_PASS * (c + 1), VU * h : VU * (h + 1), :].rearrange(
                    "(p t) v w -> p t (v w)", t=PACK
                ),
            )
            return raw

        w_raw = big.tile([P, PACK, CIN], BF16, align_bytes=64, offset=W_RAW_AT)
        f_nat = big.tile([P, S, V * T], BF16, align_bytes=64, offset=F_NAT_AT)
        for s in range(S):
            if s == W_AFTER:
                nc.sync.dma_start(
                    out=w_raw[:], in_=ada_w.rearrange("(g x) o i -> (x o) g i", x=S_BANK)
                )
            nc.sync.dma_start(out=f_nat[:, s, :], in_=feat[s].rearrange("n o w t -> (n o) (w t)"))
        raws = {(0, 0): load_ada(0, 0)}
        raws[(0, 1)] = load_ada(0, 1)
        raws[(1, 0)] = load_ada(1, 0)

        b_raw = const.tile([P, COUT], BF16)
        for s in range(S):
            nc.sync.dma_start(
                out=b_raw[W4 * s : W4 * (s + 1), :], in_=ada_b[s].partition_broadcast(W4)
            )
        pa_raw = const.tile([P, S * V], BF16)
        for half in range(2):
            nc.sync.dma_start(
                out=pa_raw[V * half : V * (half + 1), :].rearrange("v (s w) -> v s w", s=S),
                in_=PA.rearrange("s v w -> v s w"),
            )
        bn_raw = const.tile([P, 4, COUT], BF16)
        for i, vec in enumerate((bn_gamma, bn_beta, bn_mean, bn_var)):
            nc.sync.dma_start(out=bn_raw[:, i, :], in_=vec.partition_broadcast(P))
        res_view = res.rearrange("n (a h) v t -> (h v) n a t", h=2)
        out_view = out.rearrange("n (a h) v t -> (h v) n a t", h=2)

        ident = const.tile([P, P], F32)
        make_identity(nc, ident[:])
        warm = const.tile([P, 1], F32)
        nc.vector.memset(warm[:], 1.0)
        nc.scalar.activation(out=warm[:], in_=warm[:], func=ACT.Sqrt)

        def regroup_ada(raw, quad, cut):
            grouped = grouped_pool.tile([P, QUAD, VU, PACK * PACK], BF16, tag="grouped", align_bytes=64)
            dst = grouped[:].rearrange("p q v (j t) -> p v q t j", t=PACK)
            src = raw[:].rearrange("p t (v k j) -> p v k t j", v=VU, j=PACK)[
                :, :, QUAD * quad : QUAD * (quad + 1)
            ]
            nc.scalar.copy(out=dst[:, cut:], in_=src[:, cut:])
            nc.vector.tensor_copy(out=dst[:, :cut], in_=src[:, :cut])
            return grouped

        def quantise(grouped, codes, scales):
            nc.vector.quantize_mx(out=codes.bitcast(FP8X4), scales=scales, in_=grouped)

        w_words = w_raw[:].bitcast(F32).rearrange("m g (c p u) -> m g c u p", c=C_PASSES, u=2)
        w_codes = const.tile([P, C_PASSES, SO], U32, align_bytes=64)
        w_scales = const.tile([P, C_PASSES, SO], U8, align_bytes=64)

        w_tiles = []

        def prepare_w():
            for c in range(C_PASSES):
                w_grouped = grouped_pool.tile([P, SO * PACK], BF16, tag="grouped", align_bytes=64)
                w_grouped_words = w_grouped[:].bitcast(F32).rearrange("p (g m u) -> p g m u", g=PACK, u=2)
                w_tiles.append(w_grouped)
                for g_pair in range(2):
                    w_turned = ps_turn.tile([P, 4, P], F32, tag="turned")
                    for g_low in range(2):
                        for u in range(2):
                            nc.tensor.transpose(
                                w_turned[:, 2 * g_low + u, :],
                                w_words[:, 2 * g_pair + g_low, c, u, :],
                                ident[:],
                            )
                    copy_out = nc.vector.tensor_copy if g_pair == 0 else nc.scalar.copy
                    copy_out(
                        out=w_grouped_words[:, 2 * g_pair : 2 * g_pair + 2, :, :],
                        in_=w_turned[:].rearrange("p (g u) m -> p g m u", u=2),
                    )

        def quantise_w():
            for c in range(C_PASSES):
                quantise(w_tiles[c][:], w_codes[:, c, :], w_scales[:, c, :])

        pa_sorted = const.tile([P, PACK, P], F32)
        pa_t = const.tile([P, V, PACK], F32)
        b_col = const.tile([P, COUT], F32)

        def prepare_pa():
            nc.vector.tensor_copy(out=pa_sorted[:], in_=pa_raw[:].rearrange("p (k j) -> p j k", j=PACK))
            nc.vector.tensor_copy(out=b_col[:], in_=b_raw[:])
            pa_turned = ps_turn.tile([P, 4, P], F32, tag="turned")
            for j in range(PACK):
                nc.tensor.transpose(pa_turned[:, j, :], pa_sorted[:, j, :], ident[:])
            nc.vector.tensor_copy(
                out=pa_t[:], in_=pa_turned[:, :, 0:V].rearrange("p j v -> p v j")
            )

        bn_f = const.tile([P, 4, COUT], F32)
        rstd = const.tile([P, COUT], F32)
        scale_all = const.tile([P, COUT], F32)
        shift_all = const.tile([P, COUT], F32)
        scale_col = const.tile([P, COUT // 2], F32)
        shift_col = const.tile([P, COUT // 2], F32)

        def prepare_bn():
            nc.vector.tensor_copy(out=bn_f[:], in_=bn_raw[:])
            nc.vector.tensor_scalar_add(out=rstd[:], in0=bn_f[:, 3, :], scalar1=EPS)
            nc.scalar.activation(out=rstd[:], in_=rstd[:], func=ACT.Sqrt)
            nc.vector.reciprocal(out=rstd[:], in_=rstd[:])
            nc.vector.tensor_mul(out=scale_all[:], in0=bn_f[:, 0, :], in1=rstd[:])
            nc.vector.tensor_mul(out=shift_all[:], in0=bn_f[:, 2, :], in1=scale_all[:])
            nc.vector.tensor_sub(out=shift_all[:], in0=bn_f[:, 1, :], in1=shift_all[:])
            for h in range(2):
                rows = slice(V * h, V * (h + 1))
                for col, full in ((scale_col, scale_all), (shift_col, shift_all)):
                    nc.vector.tensor_copy(
                        out=col[rows, :],
                        in_=full[rows, :].rearrange("p (a h) -> p h a", h=2)[:, h, :],
                    )

        c0_codes, c1_codes = {}, {}

        def quantise_ada(c, quad, grouped):
            pool = c1_pool if c else c0_pool
            codes = pool.tile([P, ITEM], U32, tag="codes", align_bytes=64)
            scales = pool.tile([P, ITEM], U8, tag="scales", align_bytes=64)
            quantise(grouped[:].rearrange("p q v j -> p (q v j)"), codes[:], scales[:])
            (c1_codes if c else c0_codes)[quad] = (codes, scales)

        def first_matmul(quad, banks):
            unit, k = divmod(quad, QUADS)
            for bank in banks:
                acc = ps_mx.tile([P, QUAD, S_BANK * COUT], F32, tag="mx")
                n_cols = slice(P * bank, P * (bank + 1))
                for q in range(QUAD):
                    m_cols = slice(P * q, P * (q + 1))
                    for c, (codes, scales) in enumerate((c0_codes[quad], c1_codes[quad])):
                        nc.tensor.matmul_mx(
                            out=acc[:, q, :],
                            lhsT=codes[:, m_cols].bitcast(FP8X4),
                            lhsT_scale=scales[:, m_cols],
                            rhs=w_codes[:, c, n_cols].bitcast(FP8X4),
                            rhs_scale=w_scales[:, c, n_cols],
                            start=(c == 0),
                            stop=(c == C_PASSES - 1),
                        )
                nc.scalar.copy(
                    out=x_tiles[unit][
                        :, :, S_BANK * bank : S_BANK * (bank + 1), QUAD * k : QUAD * (k + 1)
                    ],
                    in_=acc[:].rearrange("p w (s o) -> p o s w", s=S_BANK),
                )

        def turn(unit, group):
            banks = []
            for half in range(2):
                turned = ps_turn.tile([P, 4, P], F32, tag="turned")
                for i in range(4):
                    nc.tensor.transpose(
                        turned[:, i, :],
                        x_tiles[unit][:, O_GROUP * group + 4 * half + i, :, :].rearrange("p s w -> p (s w)"),
                        ident[:],
                    )
                banks.append(turned)
            return banks

        def modulate(unit, group, banks, a_in):
            v0 = VU * (unit % 2)
            for half in range(2):
                for i in range(4):
                    o = O_GROUP * group + 4 * half + i
                    nc.vector.scalar_tensor_tensor(
                        out=a_in[:, o, v0 : v0 + VU, :].rearrange("p v j -> p (v j)"),
                        in0=banks[half][:, i, :],
                        scalar=b_col[:, o : o + 1],
                        in1=pa_t[:, v0 : v0 + VU, :].rearrange("p v j -> p (v j)"),
                        op0=ALU.add,
                        op1=ALU.mult,
                    )

        def quantise_a(group, a_in):
            codes = ac_pool.tile([P, O_GROUP * V], U32, tag="codes", align_bytes=64)
            scales = ac_pool.tile([P, O_GROUP * V], U8, tag="scales", align_bytes=64)
            quantise(
                a_in[:, O_GROUP * group : O_GROUP * (group + 1)].rearrange("p o v j -> p (o v j)"),
                codes[:],
                scales[:],
            )
            return codes, scales

        def sort_feat(s):
            src = f_nat[:, s, :].rearrange(
                "p (k q h e x i) -> p k h x q e i", k=W4 // SORT_LINE, q=SORT_LINE, h=2, e=2, i=4
            )
            dst = f_sorted[:, :, :, W4 * s : W4 * (s + 1), :].rearrange(
                "p h (x i) (k q) e -> p k h x q e i", q=SORT_LINE, i=4
            )
            for piece in range(2 * W4 // SORT_LINE):
                k, h = divmod(piece, 2)
                copy = nc.vector.tensor_copy if piece < SORT_V else nc.scalar.copy
                copy(out=dst[:, k, h], in_=src[:, k, h])

        def warm_up():
            bank = ps_mx.tile([P, 4, P], F32, tag="mx")
            for i in range(WARM):
                nc.tensor.matmul(
                    bank[:].rearrange("p a b -> p (a b)"),
                    lhsT=f_sorted[:, 1, T - 1, W4 * (S - 5) : W4 * (S - 1), :].rearrange("p m e -> p (m e)"),
                    rhs=f_nat[:, S - 2, 0 : 4 * P],
                    start=True,
                    stop=True,
                )

        def turn_feat(u):
            if u % 2 == 0:
                turned = ps_turn.tile([P, 4, P], F32, tag="turned")
            else:
                turned = ps_mx.tile([P, 4, P], F32, tag="mx")
            words = f_sorted[:].rearrange("p h t m e -> p h t (m e)").bitcast(F32)
            for i in range(2):
                for h in range(2):
                    nc.tensor.transpose(turned[:, 2 * i + h, :], words[:, h, 2 * u + i, :], ident[:])
            copy_out = nc.vector.tensor_copy if u % 2 == 0 else nc.scalar.copy
            copy_out(
                out=f_grouped[:]
                .rearrange("p m t j -> p (m t j)")
                .bitcast(F32)
                .rearrange("p (m x) -> p m x", m=N * COUT)[:, :, 4 * u : 4 * (u + 1)],
                in_=turned[:].rearrange("p x m -> p m x"),
            )

        def quantise_feat(chunk):
            cols = slice(O_GROUP * T * chunk, O_GROUP * T * (chunk + 1))
            quantise(
                f_grouped[:, O_GROUP * chunk : O_GROUP * (chunk + 1)].rearrange("p m t j -> p (m t j)"),
                f_codes[:, cols],
                f_scales[:, cols],
            )

        def second_matmul(n, group, a_codes):
            y_ps = ps_mx.tile([P, PAIRS, P], F32, tag="mx")
            z = z_pool.tile([P, PAIRS, T], F32)
            for pair in range(PAIRS):
                cols = slice(P * pair, P * (pair + 1))
                first = (COUT * n + O_GROUP * group) * T + P * pair
                f_cols = slice(first, first + P)
                nc.tensor.matmul_mx(
                    out=y_ps[:, pair, :],
                    lhsT=a_codes[0][:, cols].bitcast(FP8X4),
                    lhsT_scale=a_codes[1][:, cols],
                    rhs=f_codes[:, f_cols].bitcast(FP8X4),
                    rhs_scale=f_scales[:, f_cols],
                    start=True,
                    stop=True,
                )
            for h in range(2):
                rows = slice(V * h, V * (h + 1))
                for pair in range(PAIRS):
                    a = PAIRS * group + pair
                    nc.scalar.activation(
                        out=z[rows, pair, :],
                        in_=y_ps[rows, pair, T * h : T * (h + 1)],
                        func=ACT.Identity,
                        bias=shift_col[rows, a : a + 1],
                        scale=scale_col[rows, a : a + 1],
                    )
            return z

        def finish(n, group, z):
            a0 = PAIRS * group
            nc.vector.tensor_add(out=z[:], in0=z[:], in1=res_tiles[n][:, a0 : a0 + PAIRS, :])

        def store(n, group, z):
            a0 = PAIRS * group
            if n == N - 1:
                nc.scalar.activation(out=z[:], in_=z[:], func=ACT.Relu)
            else:
                nc.vector.tensor_scalar_max(out=z[:], in0=z[:], scalar1=0.0)
            nc.sync.dma_start(out=out_view[:, n, a0 : a0 + PAIRS, :], in_=z[:])

        all_quads = UNITS * QUADS
        items = [(0, 0), (0, 1)]
        for i in range(all_quads):
            items.append((0, i + 2) if i + 2 < all_quads else None)
            items.append((1, i))
        matmul_at = {}
        for i in range(all_quads):
            done = items.index((1, i)) + 1
            matmul_at[done + 1] = (i, (0, 1))
            matmul_at[done + 2] = (i, (2, 3))
        first_turn = [items.index((1, QUADS * (u + 1) - 1)) + 4 for u in range(UNITS)]
        turn_at = {}
        for u in range(UNITS):
            for g in range(GROUPS):
                turn_at[first_turn[u] + g] = (u, g)
        multiply_at = {}
        for n in range(N):
            for g in range(GROUPS):
                multiply_at[first_turn[2 * n + 1] + g + 2] = (n, g)
        ada_load_at = {}
        for u in range(1, UNITS):
            if u > 1:
                ada_load_at[items.index((1, QUADS * (u - 1) - 1)) + 1] = (u, 0)
            ada_load_at[items.index((0, QUADS * u - 1)) + 1] = (u, 1)

        res_load_at = {first_turn[0] - 4: 0, max(step for step, (n, g) in multiply_at.items() if n == 0) + 2: 1}
        res_tiles = {}
        x_tiles = {}
        a_in = None
        grouped = None
        a_codes = {}
        unfinished = None
        last = max(multiply_at)
        f_sorted = big.tile([P, 2, T, S * W4, 2], BF16, align_bytes=64, offset=F_SORTED_AT)
        for s in range(S):
            sort_feat(s)
            if s == W_AFTER:
                prepare_w()
            if s == W_AFTER + 1:
                quantise_w()
        warm_up()
        f_grouped = big.tile([P, N * COUT, T, PACK], BF16, align_bytes=64, offset=F_GROUPED_AT)
        for u in range(T // 2):
            turn_feat(u)
        f_codes = big.tile([P, N * COUT * T], U32, align_bytes=64, offset=F_CODES_AT)
        f_scales = big.tile([P, N * COUT * T], U8, align_bytes=64, offset=F_SCALES_AT)
        for step in range(last + 2):
            if step < N * COUT // O_GROUP // 2:
                quantise_feat(2 * step)
                quantise_feat(2 * step + 1)
            if step in ada_load_at:
                raws[ada_load_at[step]] = load_ada(*ada_load_at[step])
            if step in res_load_at:
                n = res_load_at[step]
                res_sb = const.tile([P, COUT // 2, T], BF16)
                nc.sync.dma_start(out=res_sb[:], in_=res_view[:, n, :, :])
                res_tiles[n] = res_sb
            if grouped is not None:
                quantise_ada(*items[step - 1], grouped)
                grouped = None
            banks = turn(*turn_at[step]) if step in turn_at else None
            if step < len(items) and items[step] is not None:
                c, quad = items[step]
                if step < N * COUT // O_GROUP // 2:
                    cut = VECTOR_V_FEAT
                else:
                    cut = VECTOR_V_ALONE if step < first_turn[0] else VECTOR_V
                grouped = regroup_ada(raws[(quad // QUADS, c)], quad % QUADS, cut)
            if step == first_turn[0] - 4:
                prepare_pa()
            if step == first_turn[0] - 2:
                prepare_bn()
            to_store = unfinished
            unfinished = None
            if to_store is not None:
                finish(*to_store)
            if step - 1 in turn_at and turn_at[step - 1][0] % 2 == 1:
                unit, g = turn_at[step - 1]
                a_codes[(unit // 2, g)] = quantise_a(g, a_in)
            if banks is not None:
                unit, g = turn_at[step]
                if unit % 2 == 0 and g == 0:
                    a_in = big.tile([P, COUT, V, PACK], BF16, align_bytes=64, offset=A_AT)
                modulate(unit, g, banks, a_in)
            if to_store is not None:
                store(*to_store)
            if step in matmul_at:
                quad, quad_banks = matmul_at[step]
                if quad % QUADS == 0 and quad_banks[0] == 0:
                    unit = quad // QUADS
                    x_sb = big.tile([P, COUT, S, W4], F32, tag=("x0", "x1")[unit % 2], align_bytes=64, offset=X_AT[unit % 2])
                    x_tiles[unit] = x_sb
                first_matmul(quad, quad_banks)
            if step in multiply_at:
                n, g = multiply_at[step]
                z = second_matmul(n, g, a_codes[(n, g)])
                unfinished = (n, g, z)
